import numpy as np
import ml_dtypes


def mxq(x, axis, fmt="e4m3"):
    dtype, down = {"e4m3": (ml_dtypes.float8_e4m3fn, 7), "e5m2": (ml_dtypes.float8_e5m2, 14)}[fmt]
    v = np.moveaxis(np.asarray(x, np.float32).astype(ml_dtypes.bfloat16).astype(np.float64), axis, -1)
    blocks = v.reshape(v.shape[:-1] + (-1, 32))
    amax = np.abs(blocks).max(-1, keepdims=True)
    byte = np.maximum(np.where(amax > 0, np.frexp(amax)[1] - 1 + 127, 0) - down, 1)
    scale = np.exp2(byte - 127.0)
    codes = (blocks / scale).astype(np.float32).astype(dtype).astype(np.float64)
    return np.moveaxis((codes * scale).reshape(v.shape), -1, axis)


WIDE = False


def mx_kscale(k):
    if not WIDE:
        return np.ones(k)
    levels = np.array([10, -10, 5, -5, 0])
    a = np.random.permutation(np.resize(levels, k // 512 * 4)).reshape(k // 512, 4)
    idx = np.arange(k)
    return np.exp2(a[idx // 512, idx % 128 // 32])


BF16 = ml_dtypes.bfloat16


def bf(x):
    return np.asarray(x, np.float32).astype(BF16)


def f64(x):
    return np.asarray(x).astype(np.float64)


B, N, R, DE, DR, NUM_BASES, OUT_DIM = 1, 1024, 16, 128, 64, 256, 128
F = DE + DR
KS = R * F


def setup_inputs():
    s = mx_kscale(N)
    t = mx_kscale(KS)[:F]
    deg = np.random.uniform(0.5, 1.5, (B, R, N, 1))
    adj = np.random.uniform(0.0, 1.0, (B, R, N, N)) * deg / np.sqrt(N)
    return {"node_features": bf(np.random.standard_normal((B, N, DE)) * 2.0 / s[:, None] * t[:DE]),
            "relation_features": bf(np.random.standard_normal((B, R, DR)) * 2.0 / np.sqrt(N) / s.mean() * t[DE:]),
            "adj": bf(adj * s),
            "Wb": bf(np.random.standard_normal((NUM_BASES, KS)) / np.sqrt(KS) / np.tile(t, R))}


def reference(node_features, relation_features, adj, Wb):
    a = f64(adj)
    node_part = mxq(a, 3, "e4m3") @ mxq(f64(node_features), 1, "e4m3")[:, None]
    row_sum = a.sum(-1)
    rel_part = row_sum[..., None] * f64(relation_features)[:, :, None, :]
    supports = np.concatenate([node_part, rel_part], -1)
    supports = supports.transpose(0, 2, 1, 3).reshape(B, N, KS)
    return mxq(supports, 2, "e4m3") @ mxq(f64(Wb), 1, "e4m3").T

@@ -1,0 +1,372 @@
+from contextlib import ExitStack
+
+import concourse.masks as masks
+import concourse.mybir as mybir
+
+F32 = mybir.dt.float32
+BF16 = mybir.dt.bfloat16
+U32 = mybir.dt.uint32
+U8 = mybir.dt.uint8
+FP8X4 = mybir.dt.float8_e4m3fn_x4
+ALU = mybir.AluOpType
+AXIS = mybir.AxisListType
+
+P = 128
+PACK = 4
+K_PASS = P * PACK
+
+NODES = 1024
+RELATIONS = 16
+D_NODE = 128
+D_REL = 64
+D_SUPPORT = D_NODE + D_REL
+BASES = 256
+BASE_HALVES = BASES // P
+
+GROUP = 4
+N_GROUPS = RELATIONS // GROUP
+N_BLOCKS = NODES // P
+N_ROUNDS = N_BLOCKS * N_GROUPS
+J_PASSES = NODES // K_PASS
+NODE_PASSES = RELATIONS * D_NODE // K_PASS
+REL_PASSES = RELATIONS * D_REL // K_PASS
+SUP_PASSES = NODE_PASSES + REL_PASSES
+
+TENSOR_SUMS = 2
+VECTOR_SUMS = GROUP - TENSOR_SUMS
+BLOCK_TENSOR_SUMS = N_GROUPS * TENSOR_SUMS
+ROWS_PER_SUM = P // PACK
+SUMS_PER_BLOCK = P // ROWS_PER_SUM
+
+QUANTISE_LAG = 1
+MULTIPLY_LAG = 2
+COLLECT_LAG = 1
+GATHER_LAG = 2
+RELATION_LAG = 3
+SUPPORT_LAG = 4
+PROJECT_LAG = 5
+WEIGHT_STEP = 2
+
+FLOPS = 2 * RELATIONS * NODES * NODES * D_NODE + 2 * NODES * RELATIONS * D_SUPPORT * BASES
+
+
+def is_round(n):
+    return 0 <= n < N_ROUNDS
+
+
+def block_ending_with(n):
+    if is_round(n) and n % N_GROUPS == N_GROUPS - 1:
+        return n // N_GROUPS
+    return None
+
+
+def tile_relationalgraphconvolution_pa_kernel(
+    tc, node_features, relation_features, adj, Wb, out
+):
+    nc = tc.nc
+    with ExitStack() as ctx:
+        ctx.enter_context(tc.manual_schedule())
+        const = ctx.enter_context(tc.tile_pool(name="const", bufs=1))
+        adj_pool = ctx.enter_context(tc.tile_pool(name="adj", bufs=4))
+        round_pool = ctx.enter_context(tc.tile_pool(name="round", bufs=3))
+        block_pool = ctx.enter_context(tc.tile_pool(name="block", bufs=2))
+        turned_psum = ctx.enter_context(tc.psum_pool(name="turned", bufs=4))
+        node_psum = ctx.enter_context(tc.psum_pool(name="node", bufs=2))
+        single_psum = ctx.enter_context(tc.psum_pool(name="single", bufs=1))
+
+        ident_f32 = const.tile([P, P], F32)
+        masks.make_identity(nc, ident_f32[:])
+        ident_bf16 = const.tile([P, P], BF16)
+        masks.make_identity(nc, ident_bf16[:])
+        ones = const.tile([P, 2], BF16)
+        nc.vector.memset(ones[:], 1.0)
+        gather = const.tile([P, SUMS_PER_BLOCK, P], F32)
+        nc.vector.memset(gather[:], 0.0)
+        for s in range(SUMS_PER_BLOCK):
+            nc.vector.tensor_reduce(
+                out=gather[:, s, s * ROWS_PER_SUM : (s + 1) * ROWS_PER_SUM],
+                in_=ident_f32[:].rearrange("k (x t) -> k x t", t=PACK),
+                axis=AXIS.X,
+                op=ALU.add,
+            )
+
+        nf_rows = const.tile([P, J_PASSES * PACK * D_NODE], BF16)
+        nc.sync.dma_start(
+            out=nf_rows[:].rearrange("p (cu ed) -> p cu ed", ed=2 * D_NODE),
+            in_=node_features[0].rearrange("(cu p e) d -> p cu (e d)", p=P, e=2),
+        )
+        nf_grouped = const.tile([P, J_PASSES, D_NODE, PACK], BF16, align_bytes=64)
+        nc.vector.tensor_copy(
+            out=nf_grouped[:],
+            in_=nf_rows[:].rearrange("p (c t d) -> p c d t", c=J_PASSES, t=PACK),
+        )
+        nf_codes = const.tile([P, J_PASSES * D_NODE], U32, align_bytes=64)
+        nf_scales = const.tile([P, J_PASSES * D_NODE], U8, align_bytes=64)
+        nc.vector.quantize_mx(
+            out=nf_codes[:].bitcast(FP8X4),
+            scales=nf_scales[:],
+            in_=nf_grouped[:].rearrange("p c d t -> p (c d t)"),
+        )
+
+        w_codes = const.tile([P, SUP_PASSES * BASES], U32, align_bytes=64)
+        w_scales = const.tile([P, SUP_PASSES * BASES], U8, align_bytes=64)
+        relf_all = const.tile([P, RELATIONS * D_REL], BF16)
+
+        def prepare_weights():
+            w_rows = const.tile([P, BASE_HALVES, RELATIONS, D_SUPPORT], BF16)
+            nc.sync.dma_start(
+                out=w_rows[:].rearrange("p h r f -> p h (r f)"),
+                in_=Wb.rearrange("(h p) k -> p h k", p=P),
+            )
+            nc.sync.dma_start(
+                out=relf_all[:],
+                in_=relation_features[0].rearrange("r e -> (r e)").partition_broadcast(P),
+            )
+            w_rel = const.tile([P, BASE_HALVES, RELATIONS * D_REL], BF16)
+            nc.vector.tensor_copy(
+                out=w_rel[:].rearrange("p h (r e) -> p h r e", e=D_REL),
+                in_=w_rows[:, :, :, D_NODE:D_SUPPORT],
+            )
+            w_grouped = const.tile([P, SUP_PASSES, BASES, PACK], BF16, align_bytes=64)
+            for q in range(SUP_PASSES):
+                w_t = turned_psum.tile([P, BASE_HALVES, PACK, P], BF16, tag="turned")
+                for h in range(BASE_HALVES):
+                    for t in range(PACK):
+                        if q < NODE_PASSES:
+                            square = w_rows[:, h, GROUP * q + t, 0:D_NODE]
+                        else:
+                            first = (q - NODE_PASSES) * K_PASS + t * P
+                            square = w_rel[:, h, first : first + P]
+                        nc.tensor.transpose(
+                            out=w_t[:, h, t, :], in_=square, identity=ident_bf16[:]
+                        )
+                copy = nc.vector.tensor_copy if q % 2 == 0 else nc.scalar.copy
+                copy(
+                    out=w_grouped[:, q].rearrange("p (h b) t -> p h b t", h=BASE_HALVES),
+                    in_=w_t[:].rearrange("p h t b -> p h b t"),
+                )
+            w_flat = w_grouped[:].rearrange("p q b t -> p (q b t)")
+            for first, width in ((0, NODE_PASSES * BASES), (NODE_PASSES * BASES, REL_PASSES * BASES)):
+                nc.vector.quantize_mx(
+                    out=w_codes[:, first : first + width].bitcast(FP8X4),
+                    scales=w_scales[:, first : first + width],
+                    in_=w_flat[:, PACK * first : PACK * (first + width)],
+                )
+
+        a_rows = {}
+        grouped = {}
+        a_codes = {}
+        a_scales = {}
+        sums_vector = {}
+        sums_psum = {}
+        sup_grouped = {}
+
+        def load_round(n):
+            block, group = divmod(n, N_GROUPS)
+            a_tile = adj_pool.tile([P, GROUP * NODES], BF16)
+            nc.sync.dma_start(
+                out=a_tile[:].rearrange("i (r j) -> i r j", r=GROUP),
+                in_=adj[
+                    0, group * GROUP : (group + 1) * GROUP, block * P : (block + 1) * P, :
+                ].rearrange("r i j -> i r j"),
+            )
+            a_rows[n] = a_tile
+
+        def sum_on_vector(n):
+            block, group = divmod(n, N_GROUPS)
+            if group == 0:
+                sums_tile = block_pool.tile([P, N_GROUPS, VECTOR_SUMS], F32)
+                sums_vector[block] = sums_tile
+            for v in range(VECTOR_SUMS):
+                r = TENSOR_SUMS + v
+                scratch = round_pool.tile([P, NODES], BF16)
+                nc.vector.tensor_scalar(
+                    out=scratch[:],
+                    in0=a_rows[n][:, r * NODES : (r + 1) * NODES],
+                    scalar1=1.0,
+                    scalar2=None,
+                    op0=ALU.mult,
+                    op1=ALU.add,
+                    accum_out=sums_vector[block][:, group, v : v + 1],
+                )
+
+        def transpose_round(n):
+            a_words = a_rows[n][:].bitcast(F32)
+            g_tile = round_pool.tile([P, GROUP * NODES], BF16, align_bytes=64)
+            g_words = g_tile[:].bitcast(F32).rearrange(
+                "p (r c i u) -> p r c i u", r=GROUP, c=J_PASSES, u=2
+            )
+            for r in range(GROUP):
+                a_t = turned_psum.tile([P, PACK, P], F32, tag="turned")
+                for cu in range(PACK):
+                    first = r * (NODES // 2) + cu * P
+                    nc.tensor.transpose(
+                        out=a_t[:, cu, :], in_=a_words[:, first : first + P], identity=ident_f32[:]
+                    )
+                nc.scalar.copy(
+                    out=g_words[:, r], in_=a_t[:].rearrange("p (c u) i -> p c i u", u=2)
+                )
+            grouped[n] = g_tile
+
+        def sum_on_tensor(n):
+            block, group = divmod(n, N_GROUPS)
+            if group == 0:
+                sums_tile = single_psum.tile([P, SUMS_PER_BLOCK * BLOCK_TENSOR_SUMS], F32)
+                sums_psum[block] = sums_tile
+            for r in range(TENSOR_SUMS):
+                for s in range(SUMS_PER_BLOCK):
+                    column = s * BLOCK_TENSOR_SUMS + group * TENSOR_SUMS + r
+                    for c in range(J_PASSES):
+                        first = ((r * J_PASSES + c) * P + s * ROWS_PER_SUM) * PACK
+                        nc.tensor.matmul(
+                            out=sums_psum[block][:, column : column + 1],
+                            lhsT=grouped[n][:, first : first + P],
+                            rhs=ones[:, 0:1],
+                            start=(c == 0),
+                            stop=(c == J_PASSES - 1),
+                        )
+
+        def quantise_round(n):
+            codes = round_pool.tile([P, GROUP * J_PASSES * P], U32, align_bytes=64)
+            scales = round_pool.tile([P, GROUP * J_PASSES * P], U8, align_bytes=64)
+            nc.vector.quantize_mx(out=codes[:].bitcast(FP8X4), scales=scales[:], in_=grouped[n][:])
+            a_codes[n] = codes
+            a_scales[n] = scales
+
+        def multiply_round(n):
+            block, group = divmod(n, N_GROUPS)
+            if group == 0:
+                sup_tile = block_pool.tile([P, SUP_PASSES, P, PACK], BF16, align_bytes=64)
+                sup_grouped[block] = sup_tile
+            node_t = node_psum.tile([P, GROUP, P], F32, tag="node")
+            for r in range(GROUP):
+                for c in range(J_PASSES):
+                    a_cols = slice((r * J_PASSES + c) * P, (r * J_PASSES + c + 1) * P)
+                    nf_cols = slice(c * D_NODE, (c + 1) * D_NODE)
+                    nc.tensor.matmul_mx(
+                        out=node_t[:, r, :],
+                        lhsT=nf_codes[:, nf_cols].bitcast(FP8X4),
+                        lhsT_scale=nf_scales[:, nf_cols],
+                        rhs=a_codes[n][:, a_cols].bitcast(FP8X4),
+                        rhs_scale=a_scales[n][:, a_cols],
+                        start=(c == 0),
+                        stop=(c == J_PASSES - 1),
+                    )
+            nc.scalar.copy(
+                out=sup_grouped[block][:, group], in_=node_t[:].rearrange("p r i -> p i r")
+            )
+
+        partial = {}
+        sums_tensor = {}
+        rel_rows = {}
+        sup_codes = {}
+        sup_scales = {}
+
+        def collect_sums(block):
+            partial_tile = block_pool.tile([P, SUMS_PER_BLOCK * BLOCK_TENSOR_SUMS], F32)
+            nc.scalar.copy(out=partial_tile[:], in_=sums_psum[block][:])
+            partial[block] = partial_tile
+
+        def gather_sums(block):
+            gathered = node_psum.tile([P, BLOCK_TENSOR_SUMS], F32, tag="node")
+            for s in range(SUMS_PER_BLOCK):
+                nc.tensor.matmul(
+                    out=gathered[:],
+                    lhsT=gather[:, s, :],
+                    rhs=partial[block][:, s * BLOCK_TENSOR_SUMS : (s + 1) * BLOCK_TENSOR_SUMS],
+                    start=(s == 0),
+                    stop=(s == SUMS_PER_BLOCK - 1),
+                )
+            sums_tensor[block] = gathered
+
+        def scale_relations(block):
+            rel_tile = block_pool.tile([P, RELATIONS * D_REL], BF16)
+            rel_view = rel_tile[:].rearrange("i (g r e) -> i g r e", g=N_GROUPS, r=GROUP)
+            relf_view = relf_all[:].rearrange("i (g r e) -> i g r e", g=N_GROUPS, r=GROUP)
+            nc.vector.tensor_tensor(
+                out=rel_view[:, :, 0:TENSOR_SUMS, :],
+                in0=relf_view[:, :, 0:TENSOR_SUMS, :],
+                in1=sums_tensor[block][:]
+                .rearrange("i (g r) -> i g r", g=N_GROUPS)
+                .unsqueeze(3)
+                .to_broadcast([P, N_GROUPS, TENSOR_SUMS, D_REL]),
+                op=ALU.mult,
+            )
+            nc.vector.tensor_tensor(
+                out=rel_view[:, :, TENSOR_SUMS:GROUP, :],
+                in0=relf_view[:, :, TENSOR_SUMS:GROUP, :],
+                in1=sums_vector[block][:]
+                .unsqueeze(3)
+                .to_broadcast([P, N_GROUPS, VECTOR_SUMS, D_REL]),
+                op=ALU.mult,
+            )
+            rel_rows[block] = rel_tile
+
+        def transpose_relations(block):
+            rel_t = turned_psum.tile([P, REL_PASSES, PACK, P], BF16, tag="turned")
+            for h in range(REL_PASSES):
+                for t in range(PACK):
+                    first = h * K_PASS + t * P
+                    nc.tensor.transpose(
+                        out=rel_t[:, h, t, :],
+                        in_=rel_rows[block][:, first : first + P],
+                        identity=ident_bf16[:],
+                    )
+            nc.scalar.copy(
+                out=sup_grouped[block][:, NODE_PASSES:SUP_PASSES],
+                in_=rel_t[:].rearrange("p h t i -> p h i t"),
+            )
+
+        def quantise_supports(block):
+            codes = block_pool.tile([P, SUP_PASSES * P], U32, align_bytes=64)
+            scales = block_pool.tile([P, SUP_PASSES * P], U8, align_bytes=64)
+            sup_flat = sup_grouped[block][:].rearrange("p q i t -> p (q i t)")
+            for first, width in ((0, NODE_PASSES * P), (NODE_PASSES * P, REL_PASSES * P)):
+                nc.vector.quantize_mx(
+                    out=codes[:, first : first + width].bitcast(FP8X4),
+                    scales=scales[:, first : first + width],
+                    in_=sup_flat[:, PACK * first : PACK * (first + width)],
+                )
+            sup_codes[block] = codes
+            sup_scales[block] = scales
+
+        def project(block):
+            out_psum = single_psum.tile([P, BASES], F32)
+            for q in range(SUP_PASSES):
+                nc.tensor.matmul_mx(
+                    out=out_psum[:],
+                    lhsT=sup_codes[block][:, q * P : (q + 1) * P].bitcast(FP8X4),
+                    lhsT_scale=sup_scales[block][:, q * P : (q + 1) * P],
+                    rhs=w_codes[:, q * BASES : (q + 1) * BASES].bitcast(FP8X4),
+                    rhs_scale=w_scales[:, q * BASES : (q + 1) * BASES],
+                    start=(q == 0),
+                    stop=(q == SUP_PASSES - 1),
+                )
+            out_rows = block_pool.tile([P, BASES], F32)
+            nc.scalar.copy(out=out_rows[:], in_=out_psum[:])
+            nc.scalar.dma_start(out=out[0, block * P : (block + 1) * P, :], in_=out_rows[:])
+
+        for step in range(N_ROUNDS + PROJECT_LAG):
+            if is_round(step):
+                load_round(step)
+                sum_on_vector(step)
+            if step == WEIGHT_STEP:
+                prepare_weights()
+            if is_round(step):
+                transpose_round(step)
+            if block_ending_with(step - RELATION_LAG) is not None:
+                transpose_relations(block_ending_with(step - RELATION_LAG))
+            if is_round(step - QUANTISE_LAG):
+                sum_on_tensor(step - QUANTISE_LAG)
+                quantise_round(step - QUANTISE_LAG)
+            if block_ending_with(step - COLLECT_LAG) is not None:
+                collect_sums(block_ending_with(step - COLLECT_LAG))
+            if block_ending_with(step - GATHER_LAG) is not None:
+                gather_sums(block_ending_with(step - GATHER_LAG))
+                scale_relations(block_ending_with(step - GATHER_LAG))
+            if block_ending_with(step - SUPPORT_LAG) is not None:
+                quantise_supports(block_ending_with(step - SUPPORT_LAG))
+            if is_round(step - MULTIPLY_LAG):
+                multiply_round(step - MULTIPLY_LAG)
+            if block_ending_with(step - PROJECT_LAG) is not None:
+                project(block_ending_with(step - PROJECT_LAG))

@@ -32,7 +32,7 @@ NODE_PASSES = RELATIONS * D_NODE // K_PASS
 REL_PASSES = RELATIONS * D_REL // K_PASS
 SUP_PASSES = NODE_PASSES + REL_PASSES
 
-TENSOR_SUMS = 2
+TENSOR_SUMS = 3
 VECTOR_SUMS = GROUP - TENSOR_SUMS
 BLOCK_TENSOR_SUMS = N_GROUPS * TENSOR_SUMS
 ROWS_PER_SUM = P // PACK
@@ -252,7 +252,7 @@ def tile_relationalgraphconvolution_pa_kernel(
                         start=(c == 0),
                         stop=(c == J_PASSES - 1),
                     )
-            nc.scalar.copy(
+            nc.vector.tensor_copy(
                 out=sup_grouped[block][:, group], in_=node_t[:].rearrange("p r i -> p i r")
             )
 

@@ -32,11 +32,12 @@ NODE_PASSES = RELATIONS * D_NODE // K_PASS
 REL_PASSES = RELATIONS * D_REL // K_PASS
 SUP_PASSES = NODE_PASSES + REL_PASSES
 
-TENSOR_SUMS = 3
+TENSOR_SUMS = 2
 VECTOR_SUMS = GROUP - TENSOR_SUMS
 BLOCK_TENSOR_SUMS = N_GROUPS * TENSOR_SUMS
 ROWS_PER_SUM = P // PACK
 SUMS_PER_BLOCK = P // ROWS_PER_SUM
+SUM_WIDTH = 32
 
 QUANTISE_LAG = 1
 MULTIPLY_LAG = 2
@@ -78,7 +79,7 @@ def tile_relationalgraphconvolution_pa_kernel(
         masks.make_identity(nc, ident_f32[:])
         ident_bf16 = const.tile([P, P], BF16)
         masks.make_identity(nc, ident_bf16[:])
-        ones = const.tile([P, 2], BF16)
+        ones = const.tile([P, SUM_WIDTH], BF16)
         nc.vector.memset(ones[:], 1.0)
         gather = const.tile([P, SUMS_PER_BLOCK, P], F32)
         nc.vector.memset(gather[:], 0.0)
@@ -211,17 +212,19 @@ def tile_relationalgraphconvolution_pa_kernel(
         def sum_on_tensor(n):
             block, group = divmod(n, N_GROUPS)
             if group == 0:
-                sums_tile = single_psum.tile([P, SUMS_PER_BLOCK * BLOCK_TENSOR_SUMS], F32)
+                sums_tile = single_psum.tile(
+                    [P, BLOCK_TENSOR_SUMS * SUMS_PER_BLOCK + SUM_WIDTH - 1], F32
+                )
                 sums_psum[block] = sums_tile
             for r in range(TENSOR_SUMS):
                 for s in range(SUMS_PER_BLOCK):
-                    column = s * BLOCK_TENSOR_SUMS + group * TENSOR_SUMS + r
+                    column = (group * TENSOR_SUMS + r) * SUMS_PER_BLOCK + s
                     for c in range(J_PASSES):
                         first = ((r * J_PASSES + c) * P + s * ROWS_PER_SUM) * PACK
                         nc.tensor.matmul(
-                            out=sums_psum[block][:, column : column + 1],
+                            out=sums_psum[block][:, column : column + SUM_WIDTH],
                             lhsT=grouped[n][:, first : first + P],
-                            rhs=ones[:, 0:1],
+                            rhs=ones[:],
                             start=(c == 0),
                             stop=(c == J_PASSES - 1),
                         )
@@ -252,7 +255,7 @@ def tile_relationalgraphconvolution_pa_kernel(
                         start=(c == 0),
                         stop=(c == J_PASSES - 1),
                     )
-            nc.vector.tensor_copy(
+            nc.scalar.copy(
                 out=sup_grouped[block][:, group], in_=node_t[:].rearrange("p r i -> p i r")
             )
 
@@ -264,7 +267,12 @@ def tile_relationalgraphconvolution_pa_kernel(
 
         def collect_sums(block):
             partial_tile = block_pool.tile([P, SUMS_PER_BLOCK * BLOCK_TENSOR_SUMS], F32)
-            nc.scalar.copy(out=partial_tile[:], in_=sums_psum[block][:])
+            nc.scalar.copy(
+                out=partial_tile[:].rearrange("k (s x) -> k s x", s=SUMS_PER_BLOCK),
+                in_=sums_psum[block][:, 0 : BLOCK_TENSOR_SUMS * SUMS_PER_BLOCK].rearrange(
+                    "k (x s) -> k s x", s=SUMS_PER_BLOCK
+                ),
+            )
             partial[block] = partial_tile
 
         def gather_sums(block):

from contextlib import ExitStack

import concourse.masks as masks
import concourse.mybir as mybir

F32 = mybir.dt.float32
BF16 = mybir.dt.bfloat16
U32 = mybir.dt.uint32
U8 = mybir.dt.uint8
FP8X4 = mybir.dt.float8_e4m3fn_x4
ALU = mybir.AluOpType
AXIS = mybir.AxisListType

P = 128
PACK = 4
K_PASS = P * PACK

NODES = 1024
RELATIONS = 16
D_NODE = 128
D_REL = 64
D_SUPPORT = D_NODE + D_REL
BASES = 256
BASE_HALVES = BASES // P

GROUP = 4
N_GROUPS = RELATIONS // GROUP
N_BLOCKS = NODES // P
N_ROUNDS = N_BLOCKS * N_GROUPS
J_PASSES = NODES // K_PASS
NODE_PASSES = RELATIONS * D_NODE // K_PASS
REL_PASSES = RELATIONS * D_REL // K_PASS
SUP_PASSES = NODE_PASSES + REL_PASSES

TENSOR_SUMS = 2
VECTOR_SUMS = GROUP - TENSOR_SUMS
BLOCK_TENSOR_SUMS = N_GROUPS * TENSOR_SUMS
ROWS_PER_SUM = P // PACK
SUMS_PER_BLOCK = P // ROWS_PER_SUM
SUM_WIDTH = 32

QUANTISE_LAG = 1
MULTIPLY_LAG = 2
COLLECT_LAG = 1
GATHER_LAG = 2
RELATION_LAG = 3
SUPPORT_LAG = 4
PROJECT_LAG = 5
WEIGHT_STEP = 2

FLOPS = 2 * RELATIONS * NODES * NODES * D_NODE + 2 * NODES * RELATIONS * D_SUPPORT * BASES


def is_round(n):
    return 0 <= n < N_ROUNDS


def block_ending_with(n):
    if is_round(n) and n % N_GROUPS == N_GROUPS - 1:
        return n // N_GROUPS
    return None


def tile_relationalgraphconvolution_pa_kernel(
    tc, node_features, relation_features, adj, Wb, out
):
    nc = tc.nc
    with ExitStack() as ctx:
        ctx.enter_context(tc.manual_schedule())
        const = ctx.enter_context(tc.tile_pool(name="const", bufs=1))
        adj_pool = ctx.enter_context(tc.tile_pool(name="adj", bufs=4))
        round_pool = ctx.enter_context(tc.tile_pool(name="round", bufs=3))
        block_pool = ctx.enter_context(tc.tile_pool(name="block", bufs=2))
        turned_psum = ctx.enter_context(tc.psum_pool(name="turned", bufs=4))
        node_psum = ctx.enter_context(tc.psum_pool(name="node", bufs=2))
        single_psum = ctx.enter_context(tc.psum_pool(name="single", bufs=1))

        ident_f32 = const.tile([P, P], F32)
        masks.make_identity(nc, ident_f32[:])
        ident_bf16 = const.tile([P, P], BF16)
        masks.make_identity(nc, ident_bf16[:])
        ones = const.tile([P, SUM_WIDTH], BF16)
        nc.vector.memset(ones[:], 1.0)
        gather = const.tile([P, SUMS_PER_BLOCK, P], F32)
        nc.vector.memset(gather[:], 0.0)
        for s in range(SUMS_PER_BLOCK):
            nc.vector.tensor_reduce(
                out=gather[:, s, s * ROWS_PER_SUM : (s + 1) * ROWS_PER_SUM],
                in_=ident_f32[:].rearrange("k (x t) -> k x t", t=PACK),
                axis=AXIS.X,
                op=ALU.add,
            )

        nf_rows = const.tile([P, J_PASSES * PACK * D_NODE], BF16)
        nc.sync.dma_start(
            out=nf_rows[:].rearrange("p (cu ed) -> p cu ed", ed=2 * D_NODE),
            in_=node_features[0].rearrange("(cu p e) d -> p cu (e d)", p=P, e=2),
        )
        nf_grouped = const.tile([P, J_PASSES, D_NODE, PACK], BF16, align_bytes=64)
        nc.vector.tensor_copy(
            out=nf_grouped[:],
            in_=nf_rows[:].rearrange("p (c t d) -> p c d t", c=J_PASSES, t=PACK),
        )
        nf_codes = const.tile([P, J_PASSES * D_NODE], U32, align_bytes=64)
        nf_scales = const.tile([P, J_PASSES * D_NODE], U8, align_bytes=64)
        nc.vector.quantize_mx(
            out=nf_codes[:].bitcast(FP8X4),
            scales=nf_scales[:],
            in_=nf_grouped[:].rearrange("p c d t -> p (c d t)"),
        )

        w_codes = const.tile([P, SUP_PASSES * BASES], U32, align_bytes=64)
        w_scales = const.tile([P, SUP_PASSES * BASES], U8, align_bytes=64)
        relf_all = const.tile([P, RELATIONS * D_REL], BF16)

        def prepare_weights():
            w_rows = const.tile([P, BASE_HALVES, RELATIONS, D_SUPPORT], BF16)
            nc.sync.dma_start(
                out=w_rows[:].rearrange("p h r f -> p h (r f)"),
                in_=Wb.rearrange("(h p) k -> p h k", p=P),
            )
            nc.sync.dma_start(
                out=relf_all[:],
                in_=relation_features[0].rearrange("r e -> (r e)").partition_broadcast(P),
            )
            w_rel = const.tile([P, BASE_HALVES, RELATIONS * D_REL], BF16)
            nc.vector.tensor_copy(
                out=w_rel[:].rearrange("p h (r e) -> p h r e", e=D_REL),
                in_=w_rows[:, :, :, D_NODE:D_SUPPORT],
            )
            w_grouped = const.tile([P, SUP_PASSES, BASES, PACK], BF16, align_bytes=64)
            for q in range(SUP_PASSES):
                w_t = turned_psum.tile([P, BASE_HALVES, PACK, P], BF16, tag="turned")
                for h in range(BASE_HALVES):
                    for t in range(PACK):
                        if q < NODE_PASSES:
                            square = w_rows[:, h, GROUP * q + t, 0:D_NODE]
                        else:
                            first = (q - NODE_PASSES) * K_PASS + t * P
                            square = w_rel[:, h, first : first + P]
                        nc.tensor.transpose(
                            out=w_t[:, h, t, :], in_=square, identity=ident_bf16[:]
                        )
                copy = nc.vector.tensor_copy if q % 2 == 0 else nc.scalar.copy
                copy(
                    out=w_grouped[:, q].rearrange("p (h b) t -> p h b t", h=BASE_HALVES),
                    in_=w_t[:].rearrange("p h t b -> p h b t"),
                )
            w_flat = w_grouped[:].rearrange("p q b t -> p (q b t)")
            for first, width in ((0, NODE_PASSES * BASES), (NODE_PASSES * BASES, REL_PASSES * BASES)):
                nc.vector.quantize_mx(
                    out=w_codes[:, first : first + width].bitcast(FP8X4),
                    scales=w_scales[:, first : first + width],
                    in_=w_flat[:, PACK * first : PACK * (first + width)],
                )

        a_rows = {}
        grouped = {}
        a_codes = {}
        a_scales = {}
        sums_vector = {}
        sums_psum = {}
        sup_grouped = {}

        def load_round(n):
            block, group = divmod(n, N_GROUPS)
            a_tile = adj_pool.tile([P, GROUP * NODES], BF16)
            nc.sync.dma_start(
                out=a_tile[:].rearrange("i (r j) -> i r j", r=GROUP),
                in_=adj[
                    0, group * GROUP : (group + 1) * GROUP, block * P : (block + 1) * P, :
                ].rearrange("r i j -> i r j"),
            )
            a_rows[n] = a_tile

        def sum_on_vector(n):
            block, group = divmod(n, N_GROUPS)
            if group == 0:
                sums_tile = block_pool.tile([P, N_GROUPS, VECTOR_SUMS], F32)
                sums_vector[block] = sums_tile
            for v in range(VECTOR_SUMS):
                r = TENSOR_SUMS + v
                scratch = round_pool.tile([P, NODES], BF16)
                nc.vector.tensor_scalar(
                    out=scratch[:],
                    in0=a_rows[n][:, r * NODES : (r + 1) * NODES],
                    scalar1=1.0,
                    scalar2=None,
                    op0=ALU.mult,
                    op1=ALU.add,
                    accum_out=sums_vector[block][:, group, v : v + 1],
                )

        def transpose_round(n):
            a_words = a_rows[n][:].bitcast(F32)
            g_tile = round_pool.tile([P, GROUP * NODES], BF16, align_bytes=64)
            g_words = g_tile[:].bitcast(F32).rearrange(
                "p (r c i u) -> p r c i u", r=GROUP, c=J_PASSES, u=2
            )
            for r in range(GROUP):
                a_t = turned_psum.tile([P, PACK, P], F32, tag="turned")
                for cu in range(PACK):
                    first = r * (NODES // 2) + cu * P
                    nc.tensor.transpose(
                        out=a_t[:, cu, :], in_=a_words[:, first : first + P], identity=ident_f32[:]
                    )
                nc.scalar.copy(
                    out=g_words[:, r], in_=a_t[:].rearrange("p (c u) i -> p c i u", u=2)
                )
            grouped[n] = g_tile

        def sum_on_tensor(n):
            block, group = divmod(n, N_GROUPS)
            if group == 0:
                sums_tile = single_psum.tile(
                    [P, BLOCK_TENSOR_SUMS * SUMS_PER_BLOCK + SUM_WIDTH - 1], F32
                )
                sums_psum[block] = sums_tile
            for r in range(TENSOR_SUMS):
                for s in range(SUMS_PER_BLOCK):
                    column = (group * TENSOR_SUMS + r) * SUMS_PER_BLOCK + s
                    for c in range(J_PASSES):
                        first = ((r * J_PASSES + c) * P + s * ROWS_PER_SUM) * PACK
                        nc.tensor.matmul(
                            out=sums_psum[block][:, column : column + SUM_WIDTH],
                            lhsT=grouped[n][:, first : first + P],
                            rhs=ones[:],
                            start=(c == 0),
                            stop=(c == J_PASSES - 1),
                        )

        def quantise_round(n):
            codes = round_pool.tile([P, GROUP * J_PASSES * P], U32, align_bytes=64)
            scales = round_pool.tile([P, GROUP * J_PASSES * P], U8, align_bytes=64)
            nc.vector.quantize_mx(out=codes[:].bitcast(FP8X4), scales=scales[:], in_=grouped[n][:])
            a_codes[n] = codes
            a_scales[n] = scales

        def multiply_round(n):
            block, group = divmod(n, N_GROUPS)
            if group == 0:
                sup_tile = block_pool.tile([P, SUP_PASSES, P, PACK], BF16, align_bytes=64)
                sup_grouped[block] = sup_tile
            node_t = node_psum.tile([P, GROUP, P], F32, tag="node")
            for r in range(GROUP):
                for c in range(J_PASSES):
                    a_cols = slice((r * J_PASSES + c) * P, (r * J_PASSES + c + 1) * P)
                    nf_cols = slice(c * D_NODE, (c + 1) * D_NODE)
                    nc.tensor.matmul_mx(
                        out=node_t[:, r, :],
                        lhsT=nf_codes[:, nf_cols].bitcast(FP8X4),
                        lhsT_scale=nf_scales[:, nf_cols],
                        rhs=a_codes[n][:, a_cols].bitcast(FP8X4),
                        rhs_scale=a_scales[n][:, a_cols],
                        start=(c == 0),
                        stop=(c == J_PASSES - 1),
                    )
            nc.scalar.copy(
                out=sup_grouped[block][:, group], in_=node_t[:].rearrange("p r i -> p i r")
            )

        partial = {}
        sums_tensor = {}
        rel_rows = {}
        sup_codes = {}
        sup_scales = {}

        def collect_sums(block):
            partial_tile = block_pool.tile([P, SUMS_PER_BLOCK * BLOCK_TENSOR_SUMS], F32)
            nc.scalar.copy(
                out=partial_tile[:].rearrange("k (s x) -> k s x", s=SUMS_PER_BLOCK),
                in_=sums_psum[block][:, 0 : BLOCK_TENSOR_SUMS * SUMS_PER_BLOCK].rearrange(
                    "k (x s) -> k s x", s=SUMS_PER_BLOCK
                ),
            )
            partial[block] = partial_tile

        def gather_sums(block):
            gathered = node_psum.tile([P, BLOCK_TENSOR_SUMS], F32, tag="node")
            for s in range(SUMS_PER_BLOCK):
                nc.tensor.matmul(
                    out=gathered[:],
                    lhsT=gather[:, s, :],
                    rhs=partial[block][:, s * BLOCK_TENSOR_SUMS : (s + 1) * BLOCK_TENSOR_SUMS],
                    start=(s == 0),
                    stop=(s == SUMS_PER_BLOCK - 1),
                )
            sums_tensor[block] = gathered

        def scale_relations(block):
            rel_tile = block_pool.tile([P, RELATIONS * D_REL], BF16)
            rel_view = rel_tile[:].rearrange("i (g r e) -> i g r e", g=N_GROUPS, r=GROUP)
            relf_view = relf_all[:].rearrange("i (g r e) -> i g r e", g=N_GROUPS, r=GROUP)
            nc.vector.tensor_tensor(
                out=rel_view[:, :, 0:TENSOR_SUMS, :],
                in0=relf_view[:, :, 0:TENSOR_SUMS, :],
                in1=sums_tensor[block][:]
                .rearrange("i (g r) -> i g r", g=N_GROUPS)
                .unsqueeze(3)
                .to_broadcast([P, N_GROUPS, TENSOR_SUMS, D_REL]),
                op=ALU.mult,
            )
            nc.vector.tensor_tensor(
                out=rel_view[:, :, TENSOR_SUMS:GROUP, :],
                in0=relf_view[:, :, TENSOR_SUMS:GROUP, :],
                in1=sums_vector[block][:]
                .unsqueeze(3)
                .to_broadcast([P, N_GROUPS, VECTOR_SUMS, D_REL]),
                op=ALU.mult,
            )
            rel_rows[block] = rel_tile

        def transpose_relations(block):
            rel_t = turned_psum.tile([P, REL_PASSES, PACK, P], BF16, tag="turned")
            for h in range(REL_PASSES):
                for t in range(PACK):
                    first = h * K_PASS + t * P
                    nc.tensor.transpose(
                        out=rel_t[:, h, t, :],
                        in_=rel_rows[block][:, first : first + P],
                        identity=ident_bf16[:],
                    )
            nc.scalar.copy(
                out=sup_grouped[block][:, NODE_PASSES:SUP_PASSES],
                in_=rel_t[:].rearrange("p h t i -> p h i t"),
            )

        def quantise_supports(block):
            codes = block_pool.tile([P, SUP_PASSES * P], U32, align_bytes=64)
            scales = block_pool.tile([P, SUP_PASSES * P], U8, align_bytes=64)
            sup_flat = sup_grouped[block][:].rearrange("p q i t -> p (q i t)")
            for first, width in ((0, NODE_PASSES * P), (NODE_PASSES * P, REL_PASSES * P)):
                nc.vector.quantize_mx(
                    out=codes[:, first : first + width].bitcast(FP8X4),
                    scales=scales[:, first : first + width],
                    in_=sup_flat[:, PACK * first : PACK * (first + width)],
                )
            sup_codes[block] = codes
            sup_scales[block] = scales

        def project(block):
            out_psum = single_psum.tile([P, BASES], F32)
            for q in range(SUP_PASSES):
                nc.tensor.matmul_mx(
                    out=out_psum[:],
                    lhsT=sup_codes[block][:, q * P : (q + 1) * P].bitcast(FP8X4),
                    lhsT_scale=sup_scales[block][:, q * P : (q + 1) * P],
                    rhs=w_codes[:, q * BASES : (q + 1) * BASES].bitcast(FP8X4),
                    rhs_scale=w_scales[:, q * BASES : (q + 1) * BASES],
                    start=(q == 0),
                    stop=(q == SUP_PASSES - 1),
                )
            out_rows = block_pool.tile([P, BASES], F32)
            nc.scalar.copy(out=out_rows[:], in_=out_psum[:])
            nc.scalar.dma_start(out=out[0, block * P : (block + 1) * P, :], in_=out_rows[:])

        for step in range(N_ROUNDS + PROJECT_LAG):
            if is_round(step):
                load_round(step)
                sum_on_vector(step)
            if step == WEIGHT_STEP:
                prepare_weights()
            if is_round(step):
                transpose_round(step)
            if block_ending_with(step - RELATION_LAG) is not None:
                transpose_relations(block_ending_with(step - RELATION_LAG))
            if is_round(step - QUANTISE_LAG):
                sum_on_tensor(step - QUANTISE_LAG)
                quantise_round(step - QUANTISE_LAG)
            if block_ending_with(step - COLLECT_LAG) is not None:
                collect_sums(block_ending_with(step - COLLECT_LAG))
            if block_ending_with(step - GATHER_LAG) is not None:
                gather_sums(block_ending_with(step - GATHER_LAG))
                scale_relations(block_ending_with(step - GATHER_LAG))
            if block_ending_with(step - SUPPORT_LAG) is not None:
                quantise_supports(block_ending_with(step - SUPPORT_LAG))
            if is_round(step - MULTIPLY_LAG):
                multiply_round(step - MULTIPLY_LAG)
            if block_ending_with(step - PROJECT_LAG) is not None:
                project(block_ending_with(step - PROJECT_LAG))
